import numpy as np
import ml_dtypes

BF16 = ml_dtypes.bfloat16


def bf(x):
    return np.asarray(x, np.float32).astype(BF16)


def f32(x):
    return np.asarray(x, np.float32)


def f64(x):
    return np.asarray(x).astype(np.float64)


def striped(idx):
    return np.tile(idx.reshape(-1, 16).T, (8, 1))


C, S, N, H = 256, 4096, 512, 4
EMB_MAX, TH_MAX = 1.5, 2.0


def pos_encoding():
    pos = f32(np.arange(N))[None, :]
    div = f32(np.exp(f64(f32(np.arange(0, C, 2)) * np.float32(-np.log(10000.0) / C))))[:, None]
    arg = f64(div * pos)
    pe = np.zeros((C, N))
    pe[0::2] = np.sin(arg)
    pe[1::2] = np.cos(arg)
    return f32(pe)


def setup_inputs():
    emb = f32(np.clip(0.5 * np.random.standard_normal((C, S)), -EMB_MAX, EMB_MAX))
    theta = f32(np.tile(np.clip(np.random.standard_normal(C // H), -TH_MAX, TH_MAX), H)[:, None])
    w = bf(0.05 * np.random.standard_normal((C, C)))
    b = f32(0.1 * np.random.standard_normal((C, 1)))
    return {"emb": emb, "pe": pos_encoding(), "theta": theta, "w": w, "b": b, "offs": striped(np.random.permutation(np.tile(np.arange(S), 2))[:N])}


def reference(emb, pe, theta, w, b, offs):
    idx = offs[:16].T.reshape(-1)
    x = f64(emb)[:, idx] + f64(pe)
    return x + f64(w).T @ np.cos(x + f64(theta)) + f64(b)

@@ -1,0 +1,62 @@
+import math
+
+import concourse.mybir as mybir
+
+P = 128
+C, S, N = 256, 4096, 512
+BLOCKS = C // P
+
+F32, BF16, U16 = mybir.dt.float32, mybir.dt.bfloat16, mybir.dt.uint16
+ADD = mybir.AluOpType.add
+ABS, SIN = mybir.ActivationFunctionType.Abs, mybir.ActivationFunctionType.Sin
+
+FLOPS = 2 * C * C * N
+
+
+def tile_qtransformertorchgen136_kernel(tc, emb, pe, theta, w, b, offs, out):
+    nc = tc.nc
+    with tc.tile_pool(name="held", bufs=1) as held, tc.psum_pool(name="psum", bufs=1) as psum:
+        offsets = held.tile([P, N // 16], U16, name="offsets")
+        nc.sync.dma_start(offsets[:], offs)
+
+        table, pos, angle, weights, bias = [], [], [], [], []
+        for k in range(BLOCKS):
+            rows = slice(k * P, (k + 1) * P)
+            table.append(held.tile([P, S], F32, name=f"table{k}"))
+            pos.append(held.tile([P, N], F32, name=f"pos{k}"))
+            angle.append(held.tile([P, 1], F32, name=f"angle{k}"))
+            weights.append(held.tile([P, C], BF16, name=f"weights{k}"))
+            bias.append(held.tile([P, 1], F32, name=f"bias{k}"))
+            nc.sync.dma_start(table[k][:], emb[rows, :])
+            nc.scalar.dma_start(pos[k][:], pe[rows, :])
+            nc.scalar.dma_start(weights[k][:], w[rows, :])
+            nc.gpsimd.dma_start(angle[k][:], theta[rows, :])
+            nc.gpsimd.dma_start(bias[k][:], b[rows, :])
+
+        half_pi = held.tile([P, 1], F32, name="half_pi")
+        nc.vector.memset(half_pi[:], math.pi / 2)
+
+        acc = [psum.tile([P, N], F32, name=f"acc{m}") for m in range(BLOCKS)]
+        x = []
+        for k in range(BLOCKS):
+            x.append(held.tile([P, N], F32, name=f"x{k}"))
+            nc.vector.tensor_tensor(x[k][:], table[k][:].indirect(offsets[:]), pos[k][:], ADD)
+
+            size = held.tile([P, N], F32, name=f"size{k}")
+            nc.scalar.activation(size[:], x[k][:], ABS, bias=angle[k][:], scale=1.0)
+            cosine = held.tile([P, N], BF16, name=f"cosine{k}")
+            nc.scalar.activation(cosine[:], size[:], SIN, bias=half_pi[:], scale=-1.0)
+
+            for m in range(BLOCKS):
+                nc.tensor.matmul(
+                    acc[m][:],
+                    weights[k][:, m * P : (m + 1) * P],
+                    cosine[:],
+                    start=(k == 0),
+                    stop=(k == BLOCKS - 1),
+                )
+
+        for m in range(BLOCKS):
+            result = held.tile([P, N], F32, name=f"result{m}")
+            nc.vector.scalar_tensor_tensor(result[:], acc[m][:], bias[m][:], x[m][:], ADD, ADD)
+            nc.sync.dma_start(out[m * P : (m + 1) * P, :], result[:])

@@ -25,13 +25,14 @@ def tile_qtransformertorchgen136_kernel(tc, emb, pe, theta, w, b, offs, out):
             table.append(held.tile([P, S], F32, name=f"table{k}"))
             pos.append(held.tile([P, N], F32, name=f"pos{k}"))
             angle.append(held.tile([P, 1], F32, name=f"angle{k}"))
-            weights.append(held.tile([P, C], BF16, name=f"weights{k}"))
             bias.append(held.tile([P, 1], F32, name=f"bias{k}"))
+            nc.sync.dma_start(pos[k][:], pe[rows, :])
             nc.sync.dma_start(table[k][:], emb[rows, :])
-            nc.scalar.dma_start(pos[k][:], pe[rows, :])
-            nc.scalar.dma_start(weights[k][:], w[rows, :])
-            nc.gpsimd.dma_start(angle[k][:], theta[rows, :])
-            nc.gpsimd.dma_start(bias[k][:], b[rows, :])
+            nc.scalar.dma_start(angle[k][:], theta[rows, :])
+            nc.scalar.dma_start(bias[k][:], b[rows, :])
+        for k in range(BLOCKS):
+            weights.append(held.tile([P, C], BF16, name=f"weights{k}"))
+            nc.sync.dma_start(weights[k][:], w[k * P : (k + 1) * P, :])
 
         half_pi = held.tile([P, 1], F32, name="half_pi")
         nc.vector.memset(half_pi[:], math.pi / 2)

@@ -5,6 +5,8 @@ import concourse.mybir as mybir
 P = 128
 C, S, N = 256, 4096, 512
 BLOCKS = C // P
+PIECES = 4
+W = N // PIECES
 
 F32, BF16, U16 = mybir.dt.float32, mybir.dt.bfloat16, mybir.dt.uint16
 ADD = mybir.AluOpType.add
@@ -37,27 +39,35 @@ def tile_qtransformertorchgen136_kernel(tc, emb, pe, theta, w, b, offs, out):
         half_pi = held.tile([P, 1], F32, name="half_pi")
         nc.vector.memset(half_pi[:], math.pi / 2)
 
-        acc = [psum.tile([P, N], F32, name=f"acc{m}") for m in range(BLOCKS)]
-        x = []
+        acc = [[psum.tile([P, W], F32, name=f"acc{m}_{i}") for i in range(PIECES)] for m in range(BLOCKS)]
+        x = [held.tile([P, N], F32, name=f"x{k}") for k in range(BLOCKS)]
+        size = [held.tile([P, N], F32, name=f"size{k}") for k in range(BLOCKS)]
+        cosine = [held.tile([P, N], BF16, name=f"cosine{k}") for k in range(BLOCKS)]
+
         for k in range(BLOCKS):
-            x.append(held.tile([P, N], F32, name=f"x{k}"))
-            nc.vector.tensor_tensor(x[k][:], table[k][:].indirect(offsets[:]), pos[k][:], ADD)
+            for i in range(PIECES):
+                cols = slice(i * W, (i + 1) * W)
+                picked = table[k][:].indirect(offsets[:, i * (W // 16) : (i + 1) * (W // 16)])
+                nc.vector.tensor_tensor(x[k][:, cols], picked, pos[k][:, cols], ADD)
 
-            size = held.tile([P, N], F32, name=f"size{k}")
-            nc.scalar.activation(size[:], x[k][:], ABS, bias=angle[k][:], scale=1.0)
-            cosine = held.tile([P, N], BF16, name=f"cosine{k}")
-            nc.scalar.activation(cosine[:], size[:], SIN, bias=half_pi[:], scale=-1.0)
+                nc.scalar.activation(size[k][:, cols], x[k][:, cols], ABS, bias=angle[k][:], scale=1.0)
+                nc.scalar.activation(cosine[k][:, cols], size[k][:, cols], SIN, bias=half_pi[:], scale=-1.0)
 
+                for m in range(BLOCKS):
+                    nc.tensor.matmul(
+                        acc[m][i][:],
+                        weights[k][:, m * P : (m + 1) * P],
+                        cosine[k][:, cols],
+                        start=(k == 0),
+                        stop=(k == BLOCKS - 1),
+                    )
+
+        result = held.tile([P, BLOCKS, N], F32, name="result")
+        out_blocks = out.rearrange("(m p) n -> p m n", p=P)
+        for i in range(PIECES):
+            cols = slice(i * W, (i + 1) * W)
             for m in range(BLOCKS):
-                nc.tensor.matmul(
-                    acc[m][:],
-                    weights[k][:, m * P : (m + 1) * P],
-                    cosine[:],
-                    start=(k == 0),
-                    stop=(k == BLOCKS - 1),
+                nc.vector.scalar_tensor_tensor(
+                    result[:, m, cols], acc[m][i][:], bias[m][:], x[m][:, cols], ADD, ADD
                 )
-
-        for m in range(BLOCKS):
-            result = held.tile([P, N], F32, name=f"result{m}")
-            nc.vector.scalar_tensor_tensor(result[:], acc[m][:], bias[m][:], x[m][:], ADD, ADD)
-            nc.sync.dma_start(out[m * P : (m + 1) * P, :], result[:])
+            nc.sync.dma_start(out_blocks[:, :, cols], result[:, :, cols])

@@ -27,14 +27,13 @@ def tile_qtransformertorchgen136_kernel(tc, emb, pe, theta, w, b, offs, out):
             table.append(held.tile([P, S], F32, name=f"table{k}"))
             pos.append(held.tile([P, N], F32, name=f"pos{k}"))
             angle.append(held.tile([P, 1], F32, name=f"angle{k}"))
+            weights.append(held.tile([P, C], BF16, name=f"weights{k}"))
             bias.append(held.tile([P, 1], F32, name=f"bias{k}"))
             nc.sync.dma_start(pos[k][:], pe[rows, :])
             nc.sync.dma_start(table[k][:], emb[rows, :])
+            nc.sync.dma_start(weights[k][:], w[rows, :])
             nc.scalar.dma_start(angle[k][:], theta[rows, :])
             nc.scalar.dma_start(bias[k][:], b[rows, :])
-        for k in range(BLOCKS):
-            weights.append(held.tile([P, C], BF16, name=f"weights{k}"))
-            nc.sync.dma_start(weights[k][:], w[k * P : (k + 1) * P, :])
 
         half_pi = held.tile([P, 1], F32, name="half_pi")
         nc.vector.memset(half_pi[:], math.pi / 2)

@@ -1,6 +1,7 @@
 import math
 
 import concourse.mybir as mybir
+from concourse.masks import make_identity
 
 P = 128
 C, S, N = 256, 4096, 512
@@ -11,6 +12,7 @@ W = N // PIECES
 F32, BF16, U16 = mybir.dt.float32, mybir.dt.bfloat16, mybir.dt.uint16
 ADD = mybir.AluOpType.add
 ABS, SIN = mybir.ActivationFunctionType.Abs, mybir.ActivationFunctionType.Sin
+IDENTITY = mybir.ActivationFunctionType.Identity
 
 FLOPS = 2 * C * C * N
 
@@ -27,16 +29,19 @@ def tile_qtransformertorchgen136_kernel(tc, emb, pe, theta, w, b, offs, out):
             table.append(held.tile([P, S], F32, name=f"table{k}"))
             pos.append(held.tile([P, N], F32, name=f"pos{k}"))
             angle.append(held.tile([P, 1], F32, name=f"angle{k}"))
-            weights.append(held.tile([P, C], BF16, name=f"weights{k}"))
             bias.append(held.tile([P, 1], F32, name=f"bias{k}"))
             nc.sync.dma_start(pos[k][:], pe[rows, :])
             nc.sync.dma_start(table[k][:], emb[rows, :])
-            nc.sync.dma_start(weights[k][:], w[rows, :])
             nc.scalar.dma_start(angle[k][:], theta[rows, :])
             nc.scalar.dma_start(bias[k][:], b[rows, :])
+        for k in range(BLOCKS):
+            weights.append(held.tile([P, C], BF16, name=f"weights{k}"))
+            nc.sync.dma_start(weights[k][:], w[k * P : (k + 1) * P, :])
 
         half_pi = held.tile([P, 1], F32, name="half_pi")
         nc.vector.memset(half_pi[:], math.pi / 2)
+        identity = held.tile([P, P], F32, name="identity")
+        make_identity(nc, identity[:])
 
         acc = [[psum.tile([P, W], F32, name=f"acc{m}_{i}") for i in range(PIECES)] for m in range(BLOCKS)]
         x = [held.tile([P, N], F32, name=f"x{k}") for k in range(BLOCKS)]
@@ -48,6 +53,8 @@ def tile_qtransformertorchgen136_kernel(tc, emb, pe, theta, w, b, offs, out):
                 cols = slice(i * W, (i + 1) * W)
                 picked = table[k][:].indirect(offsets[:, i * (W // 16) : (i + 1) * (W // 16)])
                 nc.vector.tensor_tensor(x[k][:, cols], picked, pos[k][:, cols], ADD)
+                if k == 0:
+                    nc.tensor.matmul(acc[0][i][:], identity[:], x[0][:, cols], start=True, stop=False)
 
                 nc.scalar.activation(size[k][:, cols], x[k][:, cols], ABS, bias=angle[k][:], scale=1.0)
                 nc.scalar.activation(cosine[k][:, cols], size[k][:, cols], SIN, bias=half_pi[:], scale=-1.0)
@@ -57,7 +64,7 @@ def tile_qtransformertorchgen136_kernel(tc, emb, pe, theta, w, b, offs, out):
                         acc[m][i][:],
                         weights[k][:, m * P : (m + 1) * P],
                         cosine[k][:, cols],
-                        start=(k == 0),
+                        start=(k == 0 and m != 0),
                         stop=(k == BLOCKS - 1),
                     )
 
@@ -65,8 +72,6 @@ def tile_qtransformertorchgen136_kernel(tc, emb, pe, theta, w, b, offs, out):
         out_blocks = out.rearrange("(m p) n -> p m n", p=P)
         for i in range(PIECES):
             cols = slice(i * W, (i + 1) * W)
-            for m in range(BLOCKS):
-                nc.vector.scalar_tensor_tensor(
-                    result[:, m, cols], acc[m][i][:], bias[m][:], x[m][:, cols], ADD, ADD
-                )
+            nc.scalar.activation(result[:, 0, cols], acc[0][i][:], IDENTITY, bias=bias[0][:], scale=1.0)
+            nc.vector.scalar_tensor_tensor(result[:, 1, cols], acc[1][i][:], bias[1][:], x[1][:, cols], ADD, ADD)
             nc.sync.dma_start(out_blocks[:, :, cols], result[:, :, cols])

@@ -25,18 +25,21 @@ def tile_qtransformertorchgen136_kernel(tc, emb, pe, theta, w, b, offs, out):
 
         table, pos, angle, weights, bias = [], [], [], [], []
         for k in range(BLOCKS):
-            rows = slice(k * P, (k + 1) * P)
             table.append(held.tile([P, S], F32, name=f"table{k}"))
             pos.append(held.tile([P, N], F32, name=f"pos{k}"))
             angle.append(held.tile([P, 1], F32, name=f"angle{k}"))
             bias.append(held.tile([P, 1], F32, name=f"bias{k}"))
-            nc.sync.dma_start(pos[k][:], pe[rows, :])
-            nc.sync.dma_start(table[k][:], emb[rows, :])
-            nc.scalar.dma_start(angle[k][:], theta[rows, :])
-            nc.scalar.dma_start(bias[k][:], b[rows, :])
-        for k in range(BLOCKS):
             weights.append(held.tile([P, C], BF16, name=f"weights{k}"))
-            nc.sync.dma_start(weights[k][:], w[k * P : (k + 1) * P, :])
+            nc.scalar.dma_start(angle[k][:], theta[k * P : (k + 1) * P, :])
+            nc.scalar.dma_start(bias[k][:], b[k * P : (k + 1) * P, :])
+
+        nc.sync.dma_start(pos[0][:], pe[0:P, :])
+        nc.sync.dma_start(table[0][:], emb[0:P, :])
+        nc.sync.dma_start(table[1][:], emb[P:C, :])
+        for i in range(PIECES):
+            nc.sync.dma_start(pos[1][:, i * W : (i + 1) * W], pe[P:C, i * W : (i + 1) * W])
+            if i % 2 == 1:
+                nc.sync.dma_start(weights[i // 2][:], w[(i // 2) * P : (i // 2 + 1) * P, :])
 
         half_pi = held.tile([P, 1], F32, name="half_pi")
         nc.vector.memset(half_pi[:], math.pi / 2)

@@ -36,10 +36,10 @@ def tile_qtransformertorchgen136_kernel(tc, emb, pe, theta, w, b, offs, out):
         nc.sync.dma_start(pos[0][:], pe[0:P, :])
         nc.sync.dma_start(table[0][:], emb[0:P, :])
         nc.sync.dma_start(table[1][:], emb[P:C, :])
-        for i in range(PIECES):
-            nc.sync.dma_start(pos[1][:, i * W : (i + 1) * W], pe[P:C, i * W : (i + 1) * W])
-            if i % 2 == 1:
-                nc.sync.dma_start(weights[i // 2][:], w[(i // 2) * P : (i // 2 + 1) * P, :])
+        for k in range(BLOCKS):
+            half = slice(k * (N // 2), (k + 1) * (N // 2))
+            nc.sync.dma_start(pos[1][:, half], pe[P:C, half])
+            nc.sync.dma_start(weights[k][:], w[k * P : (k + 1) * P, :])
 
         half_pi = held.tile([P, 1], F32, name="half_pi")
         nc.vector.memset(half_pi[:], math.pi / 2)

@@ -75,6 +75,9 @@ def tile_qtransformertorchgen136_kernel(tc, emb, pe, theta, w, b, offs, out):
         out_blocks = out.rearrange("(m p) n -> p m n", p=P)
         for i in range(PIECES):
             cols = slice(i * W, (i + 1) * W)
-            nc.scalar.activation(result[:, 0, cols], acc[0][i][:], IDENTITY, bias=bias[0][:], scale=1.0)
+            if i < PIECES // 2:
+                nc.vector.tensor_scalar(result[:, 0, cols], acc[0][i][:], bias[0][:], None, ADD)
+            else:
+                nc.scalar.activation(result[:, 0, cols], acc[0][i][:], IDENTITY, bias=bias[0][:], scale=1.0)
             nc.vector.scalar_tensor_tensor(result[:, 1, cols], acc[1][i][:], bias[1][:], x[1][:, cols], ADD, ADD)
             nc.sync.dma_start(out_blocks[:, :, cols], result[:, :, cols])

@@ -23,23 +23,24 @@ def tile_qtransformertorchgen136_kernel(tc, emb, pe, theta, w, b, offs, out):
         offsets = held.tile([P, N // 16], U16, name="offsets")
         nc.sync.dma_start(offsets[:], offs)
 
-        table, pos, angle, weights, bias = [], [], [], [], []
-        for k in range(BLOCKS):
-            table.append(held.tile([P, S], F32, name=f"table{k}"))
-            pos.append(held.tile([P, N], F32, name=f"pos{k}"))
-            angle.append(held.tile([P, 1], F32, name=f"angle{k}"))
-            bias.append(held.tile([P, 1], F32, name=f"bias{k}"))
-            weights.append(held.tile([P, C], BF16, name=f"weights{k}"))
-            nc.scalar.dma_start(angle[k][:], theta[k * P : (k + 1) * P, :])
-            nc.scalar.dma_start(bias[k][:], b[k * P : (k + 1) * P, :])
+        angle = held.tile([P, BLOCKS], F32, name="angle")
+        pos = held.tile([P, BLOCKS * N], F32, name="pos")
+        table = [held.tile([P, S], F32, name=f"table{k}") for k in range(BLOCKS)]
+        weights = [held.tile([P, C], BF16, name=f"weights{k}") for k in range(BLOCKS)]
+        bias = held.tile([P, BLOCKS], F32, name="bias")
+        emb_blocks = emb.rearrange("(p k) s -> k p s", k=BLOCKS)
+        w_blocks = w.rearrange("(p k) c -> k p c", k=BLOCKS)
+        pe_rows = pe.rearrange("(p k) n -> p (k n)", k=BLOCKS)
+        nc.scalar.dma_start(angle[:], theta.rearrange("(p k) o -> p (k o)", k=BLOCKS))
+        nc.scalar.dma_start(bias[:], b.rearrange("(p k) o -> p (k o)", k=BLOCKS))
 
-        nc.sync.dma_start(pos[0][:], pe[0:P, :])
-        nc.sync.dma_start(table[0][:], emb[0:P, :])
-        nc.sync.dma_start(table[1][:], emb[P:C, :])
+        early = BLOCKS * N - N // 2
+        nc.sync.dma_start(pos[:, 0:early], pe_rows[:, 0:early])
         for k in range(BLOCKS):
-            half = slice(k * (N // 2), (k + 1) * (N // 2))
-            nc.sync.dma_start(pos[1][:, half], pe[P:C, half])
-            nc.sync.dma_start(weights[k][:], w[k * P : (k + 1) * P, :])
+            nc.sync.dma_start(table[k][:], emb_blocks[k])
+        nc.sync.dma_start(weights[0][:], w_blocks[0])
+        nc.sync.dma_start(pos[:, early:], pe_rows[:, early:])
+        nc.sync.dma_start(weights[1][:], w_blocks[1])
 
         half_pi = held.tile([P, 1], F32, name="half_pi")
         nc.vector.memset(half_pi[:], math.pi / 2)
@@ -55,29 +56,29 @@ def tile_qtransformertorchgen136_kernel(tc, emb, pe, theta, w, b, offs, out):
             for i in range(PIECES):
                 cols = slice(i * W, (i + 1) * W)
                 picked = table[k][:].indirect(offsets[:, i * (W // 16) : (i + 1) * (W // 16)])
-                nc.vector.tensor_tensor(x[k][:, cols], picked, pos[k][:, cols], ADD)
+                nc.vector.tensor_tensor(x[k][:, cols], picked, pos[:, k * N + i * W : k * N + (i + 1) * W], ADD)
                 if k == 0:
                     nc.tensor.matmul(acc[0][i][:], identity[:], x[0][:, cols], start=True, stop=False)
 
-                nc.scalar.activation(size[k][:, cols], x[k][:, cols], ABS, bias=angle[k][:], scale=1.0)
+                nc.scalar.activation(size[k][:, cols], x[k][:, cols], ABS, bias=angle[:, k : k + 1], scale=1.0)
                 nc.scalar.activation(cosine[k][:, cols], size[k][:, cols], SIN, bias=half_pi[:], scale=-1.0)
 
                 for m in range(BLOCKS):
                     nc.tensor.matmul(
                         acc[m][i][:],
-                        weights[k][:, m * P : (m + 1) * P],
+                        weights[k][:, m::BLOCKS],
                         cosine[k][:, cols],
                         start=(k == 0 and m != 0),
                         stop=(k == BLOCKS - 1),
                     )
 
         result = held.tile([P, BLOCKS, N], F32, name="result")
-        out_blocks = out.rearrange("(m p) n -> p m n", p=P)
+        out_blocks = out.rearrange("(p m) n -> p m n", m=BLOCKS)
         for i in range(PIECES):
             cols = slice(i * W, (i + 1) * W)
             if i < PIECES // 2:
-                nc.vector.tensor_scalar(result[:, 0, cols], acc[0][i][:], bias[0][:], None, ADD)
+                nc.vector.tensor_scalar(result[:, 0, cols], acc[0][i][:], bias[:, 0:1], None, ADD)
             else:
-                nc.scalar.activation(result[:, 0, cols], acc[0][i][:], IDENTITY, bias=bias[0][:], scale=1.0)
-            nc.vector.scalar_tensor_tensor(result[:, 1, cols], acc[1][i][:], bias[1][:], x[1][:, cols], ADD, ADD)
+                nc.scalar.activation(result[:, 0, cols], acc[0][i][:], IDENTITY, bias=bias[:, 0:1], scale=1.0)
+            nc.vector.scalar_tensor_tensor(result[:, 1, cols], acc[1][i][:], bias[:, 1:2], x[1][:, cols], ADD, ADD)
             nc.sync.dma_start(out_blocks[:, :, cols], result[:, :, cols])

@@ -81,4 +81,6 @@ def tile_qtransformertorchgen136_kernel(tc, emb, pe, theta, w, b, offs, out):
             else:
                 nc.scalar.activation(result[:, 0, cols], acc[0][i][:], IDENTITY, bias=bias[:, 0:1], scale=1.0)
             nc.vector.scalar_tensor_tensor(result[:, 1, cols], acc[1][i][:], bias[:, 1:2], x[1][:, cols], ADD, ADD)
-            nc.sync.dma_start(out_blocks[:, :, cols], result[:, :, cols])
+            if i != PIECES - 2:
+                ready = slice((PIECES - 2) * W, N) if i == PIECES - 1 else cols
+                nc.sync.dma_start(out_blocks[:, :, ready], result[:, :, ready])

import math

import concourse.mybir as mybir
from concourse.masks import make_identity

P = 128
C, S, N = 256, 4096, 512
BLOCKS = C // P
PIECES = 4
W = N // PIECES

F32, BF16, U16 = mybir.dt.float32, mybir.dt.bfloat16, mybir.dt.uint16
ADD = mybir.AluOpType.add
ABS, SIN = mybir.ActivationFunctionType.Abs, mybir.ActivationFunctionType.Sin
IDENTITY = mybir.ActivationFunctionType.Identity

FLOPS = 2 * C * C * N


def tile_qtransformertorchgen136_kernel(tc, emb, pe, theta, w, b, offs, out):
    nc = tc.nc
    with tc.tile_pool(name="held", bufs=1) as held, tc.psum_pool(name="psum", bufs=1) as psum:
        offsets = held.tile([P, N // 16], U16, name="offsets")
        nc.sync.dma_start(offsets[:], offs)

        angle = held.tile([P, BLOCKS], F32, name="angle")
        pos = held.tile([P, BLOCKS * N], F32, name="pos")
        table = [held.tile([P, S], F32, name=f"table{k}") for k in range(BLOCKS)]
        weights = [held.tile([P, C], BF16, name=f"weights{k}") for k in range(BLOCKS)]
        bias = held.tile([P, BLOCKS], F32, name="bias")
        emb_blocks = emb.rearrange("(p k) s -> k p s", k=BLOCKS)
        w_blocks = w.rearrange("(p k) c -> k p c", k=BLOCKS)
        pe_rows = pe.rearrange("(p k) n -> p (k n)", k=BLOCKS)
        nc.scalar.dma_start(angle[:], theta.rearrange("(p k) o -> p (k o)", k=BLOCKS))
        nc.scalar.dma_start(bias[:], b.rearrange("(p k) o -> p (k o)", k=BLOCKS))

        early = BLOCKS * N - N // 2
        nc.sync.dma_start(pos[:, 0:early], pe_rows[:, 0:early])
        for k in range(BLOCKS):
            nc.sync.dma_start(table[k][:], emb_blocks[k])
        nc.sync.dma_start(weights[0][:], w_blocks[0])
        nc.sync.dma_start(pos[:, early:], pe_rows[:, early:])
        nc.sync.dma_start(weights[1][:], w_blocks[1])

        half_pi = held.tile([P, 1], F32, name="half_pi")
        nc.vector.memset(half_pi[:], math.pi / 2)
        identity = held.tile([P, P], F32, name="identity")
        make_identity(nc, identity[:])

        acc = [[psum.tile([P, W], F32, name=f"acc{m}_{i}") for i in range(PIECES)] for m in range(BLOCKS)]
        x = [held.tile([P, N], F32, name=f"x{k}") for k in range(BLOCKS)]
        size = [held.tile([P, N], F32, name=f"size{k}") for k in range(BLOCKS)]
        cosine = [held.tile([P, N], BF16, name=f"cosine{k}") for k in range(BLOCKS)]

        for k in range(BLOCKS):
            for i in range(PIECES):
                cols = slice(i * W, (i + 1) * W)
                picked = table[k][:].indirect(offsets[:, i * (W // 16) : (i + 1) * (W // 16)])
                nc.vector.tensor_tensor(x[k][:, cols], picked, pos[:, k * N + i * W : k * N + (i + 1) * W], ADD)
                if k == 0:
                    nc.tensor.matmul(acc[0][i][:], identity[:], x[0][:, cols], start=True, stop=False)

                nc.scalar.activation(size[k][:, cols], x[k][:, cols], ABS, bias=angle[:, k : k + 1], scale=1.0)
                nc.scalar.activation(cosine[k][:, cols], size[k][:, cols], SIN, bias=half_pi[:], scale=-1.0)

                for m in range(BLOCKS):
                    nc.tensor.matmul(
                        acc[m][i][:],
                        weights[k][:, m::BLOCKS],
                        cosine[k][:, cols],
                        start=(k == 0 and m != 0),
                        stop=(k == BLOCKS - 1),
                    )

        result = held.tile([P, BLOCKS, N], F32, name="result")
        out_blocks = out.rearrange("(p m) n -> p m n", m=BLOCKS)
        for i in range(PIECES):
            cols = slice(i * W, (i + 1) * W)
            if i < PIECES // 2:
                nc.vector.tensor_scalar(result[:, 0, cols], acc[0][i][:], bias[:, 0:1], None, ADD)
            else:
                nc.scalar.activation(result[:, 0, cols], acc[0][i][:], IDENTITY, bias=bias[:, 0:1], scale=1.0)
            nc.vector.scalar_tensor_tensor(result[:, 1, cols], acc[1][i][:], bias[:, 1:2], x[1][:, cols], ADD, ADD)
            if i != PIECES - 2:
                ready = slice((PIECES - 2) * W, N) if i == PIECES - 1 else cols
                nc.sync.dma_start(out_blocks[:, :, ready], result[:, :, ready])
